import numpy as np
import ml_dtypes


def mxq(x, axis, fmt="e4m3"):
    dtype, down = {"e4m3": (ml_dtypes.float8_e4m3fn, 7), "e5m2": (ml_dtypes.float8_e5m2, 14)}[fmt]
    v = np.moveaxis(np.asarray(x, np.float32).astype(ml_dtypes.bfloat16).astype(np.float64), axis, -1)
    blocks = v.reshape(v.shape[:-1] + (-1, 32))
    amax = np.abs(blocks).max(-1, keepdims=True)
    byte = np.maximum(np.where(amax > 0, np.frexp(amax)[1] - 1 + 127, 0) - down, 1)
    scale = np.exp2(byte - 127.0)
    codes = (blocks / scale).astype(np.float32).astype(dtype).astype(np.float64)
    return np.moveaxis((codes * scale).reshape(v.shape), -1, axis)


WIDE = False


def mx_kscale(k):
    if not WIDE:
        return np.ones(k)
    levels = np.array([10, -10, 5, -5, 0])
    a = np.random.permutation(np.resize(levels, k // 512 * 4)).reshape(k // 512, 4)
    idx = np.arange(k)
    return np.exp2(a[idx // 512, idx % 128 // 32])


BF16 = ml_dtypes.bfloat16


def bf(x):
    return np.asarray(x, np.float32).astype(BF16)


def f64(x):
    return np.asarray(x).astype(np.float64)


E2M1 = np.array([0.0, 0.5, 1.0, 1.5, 2.0, 3.0, 4.0, 6.0, -0.0, -0.5, -1.0, -1.5, -2.0, -3.0, -4.0, -6.0])


def pack_weight(w, fmt):
    k, n = w.shape
    w = f64(bf(w)).reshape(k // 32, 32, n)
    amax = np.abs(w).max(1)
    if fmt == "e4m3":
        byte = np.frexp(amax)[1] - 1 + 127 - 7
    else:
        mant, ex = np.frexp(amax / 6.0)
        byte = np.where(mant > 0.5, ex, ex - 1) + 127
    byte = np.clip(np.where(amax > 0, byte, 1), 1, 254)
    scaled = (w * np.exp2(127.0 - byte)[:, None, :]).reshape(k, n).astype(np.float32)
    by_word = np.ascontiguousarray(scaled.reshape(k // 512, 128, 4, n).transpose(0, 1, 3, 2))
    if fmt == "e4m3":
        words = by_word.astype(ml_dtypes.float8_e4m3fn).view(np.uint8)
    else:
        c = by_word.astype(ml_dtypes.float4_e2m1fn).view(np.uint8) & 0xF
        words = c[..., 0::2] | (c[..., 1::2] << 4)
    return np.ascontiguousarray(words), np.ascontiguousarray(byte.astype(np.uint8).reshape(k // 512, 16, n))


def unpack_weight(words, scales, fmt):
    g, p, n, _ = words.shape
    if fmt == "e4m3":
        vals = np.ascontiguousarray(words).view(ml_dtypes.float8_e4m3fn).astype(np.float64)
    else:
        nib = np.empty((g, p, n, 4), np.uint8)
        nib[..., 0::2] = words & 0xF
        nib[..., 1::2] = words >> 4
        vals = E2M1[nib]
    vals = vals * np.repeat(np.exp2(scales.astype(np.float64) - 127.0), 8, axis=1)[..., None]
    return vals.transpose(0, 1, 3, 2).reshape(g * 512, n)


B, S, D, NH, NKV, HD, QB = 1, 128, 8192, 16, 4, 128, 512
Q_DIM = NH * HD
KV_DIM = NKV * HD
FMT = "e4m3"


def rot(t, f0, f1):
    tp = t.reshape(t.shape[:-1] + (HD // 2, 2))
    t0, t1 = tp[..., 0], tp[..., 1]
    row1 = t0 * f0 + t1 * f1
    row0 = t0 * f1 - t1 * f0
    return np.stack([row0, row1], axis=-1).reshape(t.shape)


def setup_inputs():
    s = mx_kscale(D)
    x = bf(np.random.standard_normal((B, S, D)) * s)
    freqs_cis = bf(np.random.standard_normal((S, HD)))
    w = np.random.standard_normal((Q_DIM + 2 * KV_DIM, D)) / np.sqrt(D) / s
    words, scales = pack_weight(np.ascontiguousarray(w.T), FMT)
    return {"x": x,
            "freqs_cis": freqs_cis,
            "Wqkv_words": words,
            "Wqkv_scales": scales}


def reference(x, freqs_cis, Wqkv_words, Wqkv_scales):
    xqkv = mxq(f64(x), 2, "e4m3") @ unpack_weight(Wqkv_words, Wqkv_scales, FMT)
    xq = xqkv[..., :Q_DIM].reshape(B, S, NH, HD)
    xk = xqkv[..., Q_DIM:Q_DIM + KV_DIM].reshape(B, S, NKV, HD)
    xv = xqkv[..., Q_DIM + KV_DIM:].reshape(B, S, NKV, HD)
    f = f64(freqs_cis).reshape(S, 1, HD // 2, 2)
    f0, f1 = f[..., 0], f[..., 1]
    q_rot = rot(xq, f0, f1).transpose(0, 2, 1, 3)
    k_rot = rot(xk, f0, f1).transpose(0, 2, 1, 3)
    v = xv.transpose(0, 2, 1, 3)
    return q_rot, k_rot, v

@@ -1,0 +1,197 @@
+from contextlib import ExitStack
+
+import concourse.mybir as mybir
+from concourse.masks import make_identity
+
+F32 = mybir.dt.float32
+BF16 = mybir.dt.bfloat16
+I32 = mybir.dt.int32
+U8 = mybir.dt.uint8
+FP8X4 = mybir.dt.float8_e4m3fn_x4
+MULT = mybir.AluOpType.mult
+ADD = mybir.AluOpType.add
+
+P = 128
+PACK = 4
+K_PASS = P * PACK
+FEATURES = 8192
+GROUPS = FEATURES // K_PASS
+HEAD = 128
+PAIRS = HEAD // 2
+BANK = 512
+HEADS_PER_BANK = BANK // HEAD
+ROTARY_BANKS = 5
+QUERY_BANKS = 4
+ROTARY_COLS = ROTARY_BANKS * BANK
+ALL_COLS = ROTARY_COLS + BANK
+
+CHUNK_GROUPS = 4
+CHUNKS = GROUPS // CHUNK_GROUPS
+CHUNK_BANKS = 2
+BANK_GROUPS = CHUNK_GROUPS // CHUNK_BANKS
+WORDS_PER_GROUP = K_PASS // 2
+
+PLANES_PER_TILE = 4
+PLANE_TILES = GROUPS // PLANES_PER_TILE
+QUADRANTS = 4
+SCALE_ROWS = 4
+
+W_BUFS = 10
+
+FLOPS = 2 * P * FEATURES * ALL_COLS
+
+
+def tile_rlaattention_pa_k_kernel(
+    tc, x, freqs_cis, Wqkv_words, Wqkv_scales, out_0, out_1, out_2
+):
+    nc = tc.nc
+    with ExitStack() as ctx:
+        keep = ctx.enter_context(tc.tile_pool(name="keep", bufs=1))
+        x_pool = ctx.enter_context(tc.tile_pool(name="x_pool", bufs=CHUNKS))
+        grouped_pool = ctx.enter_context(tc.tile_pool(name="grouped_pool", bufs=2))
+        w_pool = ctx.enter_context(tc.tile_pool(name="w_pool", bufs=W_BUFS))
+        v_pool = ctx.enter_context(tc.tile_pool(name="v_pool", bufs=GROUPS))
+        product_pool = ctx.enter_context(tc.tile_pool(name="product_pool", bufs=2))
+        result_pool = ctx.enter_context(tc.tile_pool(name="result_pool", bufs=ROTARY_BANKS + 1))
+        psum = ctx.enter_context(tc.psum_pool(name="psum", bufs=8))
+        ctx.enter_context(tc.manual_schedule())
+
+        identity = keep.tile([P, P], F32)
+        make_identity(nc, identity[:])
+
+        planes = keep.tile([P, PLANE_TILES, ALL_COLS], U8, align_bytes=64)
+        nc.vector.memset(planes[:].bitcast(I32), 0)
+
+        x_chunks = []
+        for c in range(CHUNKS):
+            x_chunk = x_pool.tile([P, CHUNK_GROUPS * K_PASS], BF16)
+            first = c * CHUNK_GROUPS * K_PASS
+            nc.sync.dma_start(out=x_chunk[:], in_=x[0, :, first : first + CHUNK_GROUPS * K_PASS])
+            x_chunks.append(x_chunk)
+
+        for i in range(PLANE_TILES):
+            for quadrant in range(QUADRANTS):
+                nc.sync.dma_start(
+                    out=planes[32 * quadrant : 32 * quadrant + 16, i, :].bitcast(I32),
+                    in_=Wqkv_scales[
+                        PLANES_PER_TILE * i : PLANES_PER_TILE * (i + 1),
+                        SCALE_ROWS * quadrant : SCALE_ROWS * (quadrant + 1),
+                        :,
+                    ].bitcast(I32),
+                )
+
+        freqs = keep.tile([P, PAIRS, 2], BF16)
+        nc.sync.dma_start(out=freqs[:], in_=freqs_cis.rearrange("s (j e) -> s j e", e=2))
+
+        x_codes = keep.tile([P, GROUPS * P], I32, align_bytes=64)
+        x_scales = keep.tile([P, GROUPS * P], U8, align_bytes=64)
+        for c in range(CHUNKS):
+            words = x_chunks[c][:].bitcast(F32)
+            grouped = grouped_pool.tile([P, CHUNK_GROUPS * P * PACK], BF16, align_bytes=64)
+            grouped_words = grouped[:].bitcast(F32).rearrange(
+                "p (b g s u) -> p b g s u", b=CHUNK_BANKS, g=BANK_GROUPS, u=2
+            )
+            for b in range(CHUNK_BANKS):
+                transposed = psum.tile([P, BANK_GROUPS, 2, P], F32, tag="bank")
+                for g in range(BANK_GROUPS):
+                    first = (b * BANK_GROUPS + g) * WORDS_PER_GROUP
+                    for u in range(2):
+                        nc.tensor.transpose(
+                            transposed[:, g, u, :],
+                            words[:, first + u : first + WORDS_PER_GROUP : 2],
+                            identity[:],
+                        )
+                copy_out = nc.vector.tensor_copy if b == 0 else nc.scalar.copy
+                copy_out(
+                    out=grouped_words[:, b],
+                    in_=transposed[:].rearrange("p g u s -> p g s u"),
+                )
+            columns = slice(c * CHUNK_GROUPS * P, (c + 1) * CHUNK_GROUPS * P)
+            nc.vector.quantize_mx(
+                out=x_codes[:, columns].bitcast(FP8X4),
+                scales=x_scales[:, columns],
+                in_=grouped[:],
+            )
+
+        def mx_pass(acc, g, w_words, first_col):
+            i, j = divmod(g, PLANES_PER_TILE)
+            nc.tensor.matmul_mx(
+                out=acc[:],
+                lhsT=x_codes[:, g * P : (g + 1) * P].bitcast(FP8X4),
+                lhsT_scale=x_scales[:, g * P : (g + 1) * P],
+                rhs=w_words.bitcast(FP8X4),
+                rhs_scale=planes[SCALE_ROWS * j : P, i, first_col : first_col + BANK],
+                start=(g == 0),
+                stop=(g == GROUPS - 1),
+            )
+
+        rotary_acc = []
+        for b in range(ROTARY_BANKS):
+            acc = psum.tile([P, BANK], F32, tag="bank")
+            rotary_acc.append(acc)
+        for g in range(GROUPS):
+            w_rotary = w_pool.tile([P, ROTARY_COLS], I32, align_bytes=64)
+            nc.sync.dma_start(
+                out=w_rotary[:],
+                in_=Wqkv_words[g].rearrange("p n t -> p (n t)")[:, 0 : PACK * ROTARY_COLS].bitcast(I32),
+            )
+            for b in range(ROTARY_BANKS):
+                mx_pass(rotary_acc[b], g, w_rotary[:, b * BANK : (b + 1) * BANK], b * BANK)
+
+        w_values = []
+        for g in range(GROUPS):
+            w_value = v_pool.tile([P, BANK], I32, align_bytes=64)
+            nc.sync.dma_start(
+                out=w_value[:],
+                in_=Wqkv_words[g].rearrange("p n t -> p (n t)")[:, PACK * ROTARY_COLS : PACK * ALL_COLS].bitcast(I32),
+            )
+            w_values.append(w_value)
+
+        f0 = freqs[:, :, 0]
+        f1 = freqs[:, :, 1]
+        by_even = keep.tile([P, 2, PAIRS], F32)
+        by_odd = keep.tile([P, 2, PAIRS], F32)
+        nc.vector.tensor_copy(out=by_even[:, 0, :], in_=f1)
+        nc.vector.tensor_copy(out=by_even[:, 1, :], in_=f0)
+        nc.vector.tensor_scalar_mul(out=by_odd[:, 0, :], in0=f0, scalar1=-1.0)
+        nc.vector.tensor_copy(out=by_odd[:, 1, :], in_=f1)
+
+        product_shape = [P, 2, HEADS_PER_BANK, PAIRS]
+        for b in range(ROTARY_BANKS):
+            t = rotary_acc[b][:].rearrange("p (h j e) -> p h j e", h=HEADS_PER_BANK, e=2)
+            from_even = product_pool.tile(product_shape, F32)
+            nc.vector.tensor_tensor(
+                out=from_even[:],
+                in0=t[:, :, :, 0].unsqueeze(1).to_broadcast(product_shape),
+                in1=by_even[:].unsqueeze(2).to_broadcast(product_shape),
+                op=MULT,
+            )
+            from_odd = product_pool.tile(product_shape, F32)
+            nc.vector.tensor_tensor(
+                out=from_odd[:],
+                in0=t[:, :, :, 1].unsqueeze(1).to_broadcast(product_shape),
+                in1=by_odd[:].unsqueeze(2).to_broadcast(product_shape),
+                op=MULT,
+            )
+            rotated = result_pool.tile([P, HEADS_PER_BANK, PAIRS, 2], F32, tag="result")
+            nc.vector.tensor_tensor(
+                out=rotated[:],
+                in0=from_even[:].rearrange("p e h j -> p h j e"),
+                in1=from_odd[:].rearrange("p e h j -> p h j e"),
+                op=ADD,
+            )
+            if b < QUERY_BANKS:
+                heads = out_0[0, b * HEADS_PER_BANK : (b + 1) * HEADS_PER_BANK]
+            else:
+                heads = out_1[0]
+            nc.sync.dma_start(
+                out=heads.rearrange("h s f -> s h f"),
+                in_=rotated[:].rearrange("p h j e -> p h (j e)"),
+            )
+
+        value_acc = psum.tile([P, BANK], F32, tag="bank")
+        for g in range(GROUPS):
+            mx_pass(value_acc, g, w_values[g][:], ROTARY_COLS)
+        values = result_pool.tile([P, HEADS_PER_BANK, HEAD], F32, tag="result")
+        nc.scalar.copy(out=values[:], in_=value_acc[:].rearrange("p (h f) -> p h f", h=HEADS_PER_BANK))
+        nc.sync.dma_start(out=out_2[0].rearrange("h s f -> s h f"), in_=values[:])

@@ -71,13 +71,13 @@ def tile_rlaattention_pa_k_kernel(
 
         for i in range(PLANE_TILES):
             for quadrant in range(QUADRANTS):
-                nc.sync.dma_start(
-                    out=planes[32 * quadrant : 32 * quadrant + 16, i, :].bitcast(I32),
+                nc.gpsimd.dma_start(
+                    out=planes[32 * quadrant : 32 * quadrant + 16, i, :].bitcast(F32),
                     in_=Wqkv_scales[
                         PLANES_PER_TILE * i : PLANES_PER_TILE * (i + 1),
                         SCALE_ROWS * quadrant : SCALE_ROWS * (quadrant + 1),
                         :,
-                    ].bitcast(I32),
+                    ].bitcast(F32),
                 )
 
         freqs = keep.tile([P, PAIRS, 2], BF16)

@@ -33,6 +33,7 @@ WORDS_PER_GROUP = K_PASS // 2
 
 PLANES_PER_TILE = 4
 PLANE_TILES = GROUPS // PLANES_PER_TILE
+SYNC_TILES = 2
 QUADRANTS = 4
 SCALE_ROWS = 4
 
@@ -60,7 +61,19 @@ def tile_rlaattention_pa_k_kernel(
         make_identity(nc, identity[:])
 
         planes = keep.tile([P, PLANE_TILES, ALL_COLS], U8, align_bytes=64)
-        nc.vector.memset(planes[:].bitcast(I32), 0)
+        for i in range(PLANE_TILES):
+            nc.vector.memset(planes[:, i, :].bitcast(I32), 0)
+
+        def load_planes(queue, i, view):
+            for quadrant in range(QUADRANTS):
+                queue.dma_start(
+                    out=planes[32 * quadrant : 32 * quadrant + 16, i, :].bitcast(view),
+                    in_=Wqkv_scales[
+                        PLANES_PER_TILE * i : PLANES_PER_TILE * (i + 1),
+                        SCALE_ROWS * quadrant : SCALE_ROWS * (quadrant + 1),
+                        :,
+                    ].bitcast(view),
+                )
 
         x_chunks = []
         for c in range(CHUNKS):
@@ -69,19 +82,13 @@ def tile_rlaattention_pa_k_kernel(
             nc.sync.dma_start(out=x_chunk[:], in_=x[0, :, first : first + CHUNK_GROUPS * K_PASS])
             x_chunks.append(x_chunk)
 
-        for i in range(PLANE_TILES):
-            for quadrant in range(QUADRANTS):
-                nc.gpsimd.dma_start(
-                    out=planes[32 * quadrant : 32 * quadrant + 16, i, :].bitcast(F32),
-                    in_=Wqkv_scales[
-                        PLANES_PER_TILE * i : PLANES_PER_TILE * (i + 1),
-                        SCALE_ROWS * quadrant : SCALE_ROWS * (quadrant + 1),
-                        :,
-                    ].bitcast(F32),
-                )
+        for i in range(SYNC_TILES):
+            load_planes(nc.sync, i, I32)
+        for i in range(SYNC_TILES, PLANE_TILES):
+            load_planes(nc.gpsimd, i, F32)
 
         freqs = keep.tile([P, PAIRS, 2], BF16)
-        nc.sync.dma_start(out=freqs[:], in_=freqs_cis.rearrange("s (j e) -> s j e", e=2))
+        nc.gpsimd.dma_start(out=freqs[:], in_=freqs_cis.rearrange("s (j e) -> s j e", e=2))
 
         x_codes = keep.tile([P, GROUPS * P], I32, align_bytes=64)
         x_scales = keep.tile([P, GROUPS * P], U8, align_bytes=64)

@@ -22,8 +22,8 @@ BANK = 512
 HEADS_PER_BANK = BANK // HEAD
 ROTARY_BANKS = 5
 QUERY_BANKS = 4
-ROTARY_COLS = ROTARY_BANKS * BANK
-ALL_COLS = ROTARY_COLS + BANK
+ALL_BANKS = ROTARY_BANKS + 1
+ALL_COLS = ALL_BANKS * BANK
 
 CHUNK_GROUPS = 4
 CHUNKS = GROUPS // CHUNK_GROUPS
@@ -37,7 +37,11 @@ SYNC_TILES = 2
 QUADRANTS = 4
 SCALE_ROWS = 4
 
-W_BUFS = 10
+W_BUFS = 14
+PAIR = 2
+LAST_START = 10
+KEY_LOADS = ((10, 14), (14, 16))
+VALUE_LOADS = ((10, 14), (14, 15), (15, 16))
 
 FLOPS = 2 * P * FEATURES * ALL_COLS
 
@@ -51,7 +55,7 @@ def tile_rlaattention_pa_k_kernel(
         x_pool = ctx.enter_context(tc.tile_pool(name="x_pool", bufs=CHUNKS))
         grouped_pool = ctx.enter_context(tc.tile_pool(name="grouped_pool", bufs=2))
         w_pool = ctx.enter_context(tc.tile_pool(name="w_pool", bufs=W_BUFS))
-        v_pool = ctx.enter_context(tc.tile_pool(name="v_pool", bufs=GROUPS))
+        last_pool = ctx.enter_context(tc.tile_pool(name="last_pool", bufs=1))
         product_pool = ctx.enter_context(tc.tile_pool(name="product_pool", bufs=2))
         result_pool = ctx.enter_context(tc.tile_pool(name="result_pool", bufs=ROTARY_BANKS + 1))
         psum = ctx.enter_context(tc.psum_pool(name="psum", bufs=8))
@@ -132,27 +136,23 @@ def tile_rlaattention_pa_k_kernel(
                 stop=(g == GROUPS - 1),
             )
 
-        rotary_acc = []
-        for b in range(ROTARY_BANKS):
-            acc = psum.tile([P, BANK], F32, tag="bank")
-            rotary_acc.append(acc)
-        for g in range(GROUPS):
-            w_rotary = w_pool.tile([P, ROTARY_COLS], I32, align_bytes=64)
+        def load(pool, name, groups, banks):
+            first, end = groups
+            low, high = banks
+            tile = pool.tile([P, end - first, (high - low) * BANK], I32, align_bytes=64, name=name)
             nc.sync.dma_start(
-                out=w_rotary[:],
-                in_=Wqkv_words[g].rearrange("p n t -> p (n t)")[:, 0 : PACK * ROTARY_COLS].bitcast(I32),
+                out=tile[:],
+                in_=Wqkv_words[first:end]
+                .rearrange("g p n t -> p g (n t)")[:, :, PACK * low * BANK : PACK * high * BANK]
+                .bitcast(I32),
             )
-            for b in range(ROTARY_BANKS):
-                mx_pass(rotary_acc[b], g, w_rotary[:, b * BANK : (b + 1) * BANK], b * BANK)
+            return tile
 
-        w_values = []
-        for g in range(GROUPS):
-            w_value = v_pool.tile([P, BANK], I32, align_bytes=64)
-            nc.sync.dma_start(
-                out=w_value[:],
-                in_=Wqkv_words[g].rearrange("p n t -> p (n t)")[:, PACK * ROTARY_COLS : PACK * ALL_COLS].bitcast(I32),
-            )
-            w_values.append(w_value)
+        def passes(tile, groups, banks):
+            for b in range(banks[0], banks[1]):
+                for g in range(groups[0], groups[1]):
+                    col = (b - banks[0]) * BANK
+                    mx_pass(accs[b], g, tile[:, g - groups[0], col : col + BANK], b * BANK)
 
         f0 = freqs[:, :, 0]
         f1 = freqs[:, :, 1]
@@ -164,8 +164,10 @@ def tile_rlaattention_pa_k_kernel(
         nc.vector.tensor_copy(out=by_odd[:, 1, :], in_=f1)
 
         product_shape = [P, 2, HEADS_PER_BANK, PAIRS]
-        for b in range(ROTARY_BANKS):
-            t = rotary_acc[b][:].rearrange("p (h j e) -> p h j e", h=HEADS_PER_BANK, e=2)
+        results = []
+
+        def rotate(b):
+            t = accs[b][:].rearrange("p (h j e) -> p h j e", h=HEADS_PER_BANK, e=2)
             from_even = product_pool.tile(product_shape, F32)
             nc.vector.tensor_tensor(
                 out=from_even[:],
@@ -187,18 +189,47 @@ def tile_rlaattention_pa_k_kernel(
                 in1=from_odd[:].rearrange("p e h j -> p h j e"),
                 op=ADD,
             )
+            results.append(rotated)
+
+        def store(b):
             if b < QUERY_BANKS:
                 heads = out_0[0, b * HEADS_PER_BANK : (b + 1) * HEADS_PER_BANK]
             else:
                 heads = out_1[0]
             nc.sync.dma_start(
                 out=heads.rearrange("h s f -> s h f"),
-                in_=rotated[:].rearrange("p h j e -> p h (j e)"),
+                in_=results[b][:].rearrange("p h j e -> p h (j e)"),
             )
 
-        value_acc = psum.tile([P, BANK], F32, tag="bank")
+        accs = []
+        for b in range(ALL_BANKS):
+            acc = psum.tile([P, BANK], F32, tag="bank")
+            accs.append(acc)
+
+        banks = (0, QUERY_BANKS)
         for g in range(GROUPS):
-            mx_pass(value_acc, g, w_values[g][:], ROTARY_COLS)
+            groups = (g, g + 1)
+            passes(load(w_pool, "w_whole", groups, banks), groups, banks)
+        for b in range(QUERY_BANKS):
+            rotate(b)
+
+        banks = (QUERY_BANKS, ALL_BANKS)
+        for first in range(0, LAST_START, PAIR):
+            groups = (first, first + PAIR)
+            passes(load(w_pool, "w_whole", groups, banks), groups, banks)
+
+        key_banks = (QUERY_BANKS, ROTARY_BANKS)
+        value_banks = (ROTARY_BANKS, ALL_BANKS)
+        w_keys = [load(last_pool, "w_keys_%d" % r[0], r, key_banks) for r in KEY_LOADS]
+        w_values = [load(last_pool, "w_values_%d" % r[0], r, value_banks) for r in VALUE_LOADS]
+        for b in range(QUERY_BANKS):
+            store(b)
+        for r, tile in zip(KEY_LOADS, w_keys):
+            passes(tile, r, key_banks)
+        rotate(QUERY_BANKS)
+        store(QUERY_BANKS)
+        for r, tile in zip(VALUE_LOADS, w_values):
+            passes(tile, r, value_banks)
         values = result_pool.tile([P, HEADS_PER_BANK, HEAD], F32, tag="result")
-        nc.scalar.copy(out=values[:], in_=value_acc[:].rearrange("p (h f) -> p h f", h=HEADS_PER_BANK))
-        nc.sync.dma_start(out=out_2[0].rearrange("h s f -> s h f"), in_=values[:])
+        nc.scalar.copy(out=values[:], in_=accs[ROTARY_BANKS][:].rearrange("p (h f) -> p h f", h=HEADS_PER_BANK))
+        nc.scalar.dma_start(out=out_2[0].rearrange("h s f -> s h f"), in_=values[:])

from contextlib import ExitStack

import concourse.mybir as mybir
from concourse.masks import make_identity

F32 = mybir.dt.float32
BF16 = mybir.dt.bfloat16
I32 = mybir.dt.int32
U8 = mybir.dt.uint8
FP8X4 = mybir.dt.float8_e4m3fn_x4
MULT = mybir.AluOpType.mult
ADD = mybir.AluOpType.add

P = 128
PACK = 4
K_PASS = P * PACK
FEATURES = 8192
GROUPS = FEATURES // K_PASS
HEAD = 128
PAIRS = HEAD // 2
BANK = 512
HEADS_PER_BANK = BANK // HEAD
ROTARY_BANKS = 5
QUERY_BANKS = 4
ALL_BANKS = ROTARY_BANKS + 1
ALL_COLS = ALL_BANKS * BANK

CHUNK_GROUPS = 4
CHUNKS = GROUPS // CHUNK_GROUPS
CHUNK_BANKS = 2
BANK_GROUPS = CHUNK_GROUPS // CHUNK_BANKS
WORDS_PER_GROUP = K_PASS // 2

PLANES_PER_TILE = 4
PLANE_TILES = GROUPS // PLANES_PER_TILE
SYNC_TILES = 2
QUADRANTS = 4
SCALE_ROWS = 4

W_BUFS = 14
PAIR = 2
LAST_START = 10
KEY_LOADS = ((10, 14), (14, 16))
VALUE_LOADS = ((10, 14), (14, 15), (15, 16))

FLOPS = 2 * P * FEATURES * ALL_COLS


def tile_rlaattention_pa_k_kernel(
    tc, x, freqs_cis, Wqkv_words, Wqkv_scales, out_0, out_1, out_2
):
    nc = tc.nc
    with ExitStack() as ctx:
        keep = ctx.enter_context(tc.tile_pool(name="keep", bufs=1))
        x_pool = ctx.enter_context(tc.tile_pool(name="x_pool", bufs=CHUNKS))
        grouped_pool = ctx.enter_context(tc.tile_pool(name="grouped_pool", bufs=2))
        w_pool = ctx.enter_context(tc.tile_pool(name="w_pool", bufs=W_BUFS))
        last_pool = ctx.enter_context(tc.tile_pool(name="last_pool", bufs=1))
        product_pool = ctx.enter_context(tc.tile_pool(name="product_pool", bufs=2))
        result_pool = ctx.enter_context(tc.tile_pool(name="result_pool", bufs=ROTARY_BANKS + 1))
        psum = ctx.enter_context(tc.psum_pool(name="psum", bufs=8))
        ctx.enter_context(tc.manual_schedule())

        identity = keep.tile([P, P], F32)
        make_identity(nc, identity[:])

        planes = keep.tile([P, PLANE_TILES, ALL_COLS], U8, align_bytes=64)
        for i in range(PLANE_TILES):
            nc.vector.memset(planes[:, i, :].bitcast(I32), 0)

        def load_planes(queue, i, view):
            for quadrant in range(QUADRANTS):
                queue.dma_start(
                    out=planes[32 * quadrant : 32 * quadrant + 16, i, :].bitcast(view),
                    in_=Wqkv_scales[
                        PLANES_PER_TILE * i : PLANES_PER_TILE * (i + 1),
                        SCALE_ROWS * quadrant : SCALE_ROWS * (quadrant + 1),
                        :,
                    ].bitcast(view),
                )

        x_chunks = []
        for c in range(CHUNKS):
            x_chunk = x_pool.tile([P, CHUNK_GROUPS * K_PASS], BF16)
            first = c * CHUNK_GROUPS * K_PASS
            nc.sync.dma_start(out=x_chunk[:], in_=x[0, :, first : first + CHUNK_GROUPS * K_PASS])
            x_chunks.append(x_chunk)

        for i in range(SYNC_TILES):
            load_planes(nc.sync, i, I32)
        for i in range(SYNC_TILES, PLANE_TILES):
            load_planes(nc.gpsimd, i, F32)

        freqs = keep.tile([P, PAIRS, 2], BF16)
        nc.gpsimd.dma_start(out=freqs[:], in_=freqs_cis.rearrange("s (j e) -> s j e", e=2))

        x_codes = keep.tile([P, GROUPS * P], I32, align_bytes=64)
        x_scales = keep.tile([P, GROUPS * P], U8, align_bytes=64)
        for c in range(CHUNKS):
            words = x_chunks[c][:].bitcast(F32)
            grouped = grouped_pool.tile([P, CHUNK_GROUPS * P * PACK], BF16, align_bytes=64)
            grouped_words = grouped[:].bitcast(F32).rearrange(
                "p (b g s u) -> p b g s u", b=CHUNK_BANKS, g=BANK_GROUPS, u=2
            )
            for b in range(CHUNK_BANKS):
                transposed = psum.tile([P, BANK_GROUPS, 2, P], F32, tag="bank")
                for g in range(BANK_GROUPS):
                    first = (b * BANK_GROUPS + g) * WORDS_PER_GROUP
                    for u in range(2):
                        nc.tensor.transpose(
                            transposed[:, g, u, :],
                            words[:, first + u : first + WORDS_PER_GROUP : 2],
                            identity[:],
                        )
                copy_out = nc.vector.tensor_copy if b == 0 else nc.scalar.copy
                copy_out(
                    out=grouped_words[:, b],
                    in_=transposed[:].rearrange("p g u s -> p g s u"),
                )
            columns = slice(c * CHUNK_GROUPS * P, (c + 1) * CHUNK_GROUPS * P)
            nc.vector.quantize_mx(
                out=x_codes[:, columns].bitcast(FP8X4),
                scales=x_scales[:, columns],
                in_=grouped[:],
            )

        def mx_pass(acc, g, w_words, first_col):
            i, j = divmod(g, PLANES_PER_TILE)
            nc.tensor.matmul_mx(
                out=acc[:],
                lhsT=x_codes[:, g * P : (g + 1) * P].bitcast(FP8X4),
                lhsT_scale=x_scales[:, g * P : (g + 1) * P],
                rhs=w_words.bitcast(FP8X4),
                rhs_scale=planes[SCALE_ROWS * j : P, i, first_col : first_col + BANK],
                start=(g == 0),
                stop=(g == GROUPS - 1),
            )

        def load(pool, name, groups, banks):
            first, end = groups
            low, high = banks
            tile = pool.tile([P, end - first, (high - low) * BANK], I32, align_bytes=64, name=name)
            nc.sync.dma_start(
                out=tile[:],
                in_=Wqkv_words[first:end]
                .rearrange("g p n t -> p g (n t)")[:, :, PACK * low * BANK : PACK * high * BANK]
                .bitcast(I32),
            )
            return tile

        def passes(tile, groups, banks):
            for b in range(banks[0], banks[1]):
                for g in range(groups[0], groups[1]):
                    col = (b - banks[0]) * BANK
                    mx_pass(accs[b], g, tile[:, g - groups[0], col : col + BANK], b * BANK)

        f0 = freqs[:, :, 0]
        f1 = freqs[:, :, 1]
        by_even = keep.tile([P, 2, PAIRS], F32)
        by_odd = keep.tile([P, 2, PAIRS], F32)
        nc.vector.tensor_copy(out=by_even[:, 0, :], in_=f1)
        nc.vector.tensor_copy(out=by_even[:, 1, :], in_=f0)
        nc.vector.tensor_scalar_mul(out=by_odd[:, 0, :], in0=f0, scalar1=-1.0)
        nc.vector.tensor_copy(out=by_odd[:, 1, :], in_=f1)

        product_shape = [P, 2, HEADS_PER_BANK, PAIRS]
        results = []

        def rotate(b):
            t = accs[b][:].rearrange("p (h j e) -> p h j e", h=HEADS_PER_BANK, e=2)
            from_even = product_pool.tile(product_shape, F32)
            nc.vector.tensor_tensor(
                out=from_even[:],
                in0=t[:, :, :, 0].unsqueeze(1).to_broadcast(product_shape),
                in1=by_even[:].unsqueeze(2).to_broadcast(product_shape),
                op=MULT,
            )
            from_odd = product_pool.tile(product_shape, F32)
            nc.vector.tensor_tensor(
                out=from_odd[:],
                in0=t[:, :, :, 1].unsqueeze(1).to_broadcast(product_shape),
                in1=by_odd[:].unsqueeze(2).to_broadcast(product_shape),
                op=MULT,
            )
            rotated = result_pool.tile([P, HEADS_PER_BANK, PAIRS, 2], F32, tag="result")
            nc.vector.tensor_tensor(
                out=rotated[:],
                in0=from_even[:].rearrange("p e h j -> p h j e"),
                in1=from_odd[:].rearrange("p e h j -> p h j e"),
                op=ADD,
            )
            results.append(rotated)

        def store(b):
            if b < QUERY_BANKS:
                heads = out_0[0, b * HEADS_PER_BANK : (b + 1) * HEADS_PER_BANK]
            else:
                heads = out_1[0]
            nc.sync.dma_start(
                out=heads.rearrange("h s f -> s h f"),
                in_=results[b][:].rearrange("p h j e -> p h (j e)"),
            )

        accs = []
        for b in range(ALL_BANKS):
            acc = psum.tile([P, BANK], F32, tag="bank")
            accs.append(acc)

        banks = (0, QUERY_BANKS)
        for g in range(GROUPS):
            groups = (g, g + 1)
            passes(load(w_pool, "w_whole", groups, banks), groups, banks)
        for b in range(QUERY_BANKS):
            rotate(b)

        banks = (QUERY_BANKS, ALL_BANKS)
        for first in range(0, LAST_START, PAIR):
            groups = (first, first + PAIR)
            passes(load(w_pool, "w_whole", groups, banks), groups, banks)

        key_banks = (QUERY_BANKS, ROTARY_BANKS)
        value_banks = (ROTARY_BANKS, ALL_BANKS)
        w_keys = [load(last_pool, "w_keys_%d" % r[0], r, key_banks) for r in KEY_LOADS]
        w_values = [load(last_pool, "w_values_%d" % r[0], r, value_banks) for r in VALUE_LOADS]
        for b in range(QUERY_BANKS):
            store(b)
        for r, tile in zip(KEY_LOADS, w_keys):
            passes(tile, r, key_banks)
        rotate(QUERY_BANKS)
        store(QUERY_BANKS)
        for r, tile in zip(VALUE_LOADS, w_values):
            passes(tile, r, value_banks)
        values = result_pool.tile([P, HEADS_PER_BANK, HEAD], F32, tag="result")
        nc.scalar.copy(out=values[:], in_=accs[ROTARY_BANKS][:].rearrange("p (h f) -> p h f", h=HEADS_PER_BANK))
        nc.scalar.dma_start(out=out_2[0].rearrange("h s f -> s h f"), in_=values[:])
